import numpy as np
import ml_dtypes


def mxq(x, axis, fmt="e4m3"):
    dtype, down = {"e4m3": (ml_dtypes.float8_e4m3fn, 7), "e5m2": (ml_dtypes.float8_e5m2, 14)}[fmt]
    v = np.moveaxis(np.asarray(x, np.float32).astype(ml_dtypes.bfloat16).astype(np.float64), axis, -1)
    blocks = v.reshape(v.shape[:-1] + (-1, 32))
    amax = np.abs(blocks).max(-1, keepdims=True)
    byte = np.maximum(np.where(amax > 0, np.frexp(amax)[1] - 1 + 127, 0) - down, 1)
    scale = np.exp2(byte - 127.0)
    codes = (blocks / scale).astype(np.float32).astype(dtype).astype(np.float64)
    return np.moveaxis((codes * scale).reshape(v.shape), -1, axis)


WIDE = False


def mx_kscale(k):
    if not WIDE:
        return np.ones(k)
    levels = np.array([10, -10, 5, -5, 0])
    a = np.random.permutation(np.resize(levels, k // 512 * 4)).reshape(k // 512, 4)
    idx = np.arange(k)
    return np.exp2(a[idx // 512, idx % 128 // 32])


BF16 = ml_dtypes.bfloat16


def bf(x):
    return np.asarray(x, np.float32).astype(BF16)


def f64(x):
    return np.asarray(x).astype(np.float64)


E2M1 = np.array([0.0, 0.5, 1.0, 1.5, 2.0, 3.0, 4.0, 6.0, -0.0, -0.5, -1.0, -1.5, -2.0, -3.0, -4.0, -6.0])


def pack_weight(w, fmt):
    k, n = w.shape
    w = f64(bf(w)).reshape(k // 32, 32, n)
    amax = np.abs(w).max(1)
    if fmt == "e4m3":
        byte = np.frexp(amax)[1] - 1 + 127 - 7
    else:
        mant, ex = np.frexp(amax / 6.0)
        byte = np.where(mant > 0.5, ex, ex - 1) + 127
    byte = np.clip(np.where(amax > 0, byte, 1), 1, 254)
    scaled = (w * np.exp2(127.0 - byte)[:, None, :]).reshape(k, n).astype(np.float32)
    by_word = np.ascontiguousarray(scaled.reshape(k // 512, 128, 4, n).transpose(0, 1, 3, 2))
    if fmt == "e4m3":
        words = by_word.astype(ml_dtypes.float8_e4m3fn).view(np.uint8)
    else:
        c = by_word.astype(ml_dtypes.float4_e2m1fn).view(np.uint8) & 0xF
        words = c[..., 0::2] | (c[..., 1::2] << 4)
    return np.ascontiguousarray(words), np.ascontiguousarray(byte.astype(np.uint8).reshape(k // 512, 16, n))


def unpack_weight(words, scales, fmt):
    g, p, n, _ = words.shape
    if fmt == "e4m3":
        vals = np.ascontiguousarray(words).view(ml_dtypes.float8_e4m3fn).astype(np.float64)
    else:
        nib = np.empty((g, p, n, 4), np.uint8)
        nib[..., 0::2] = words & 0xF
        nib[..., 1::2] = words >> 4
        vals = E2M1[nib]
    vals = vals * np.repeat(np.exp2(scales.astype(np.float64) - 127.0), 8, axis=1)[..., None]
    return vals.transpose(0, 1, 3, 2).reshape(g * 512, n)


B, N, NIN, CTX, H, NOUT = 8, 512, 512, 3, 512, 2
F = NIN * CTX


def shift_down(y, d):
    return np.pad(y[:, :-d, :], ((0, 0), (d, 0), (0, 0)))


def shift_up(y, d):
    return np.pad(y[:, d:, :], ((0, 0), (0, d), (0, 0)))


def context_linear(xq, wt, shifts):
    y = xq @ wt[:NIN]
    c = 1
    for d in range(1, CTX // 2 + 1):
        for shift in shifts:
            y = y + shift(xq @ wt[c * NIN:(c + 1) * NIN], d)
            c += 1
    return y


def setup_inputs():
    s, u = mx_kscale(NIN), mx_kscale(H)
    x_l = bf(np.random.standard_normal((B, N, NIN)) * s)
    w_l = np.random.standard_normal((H, F)) / np.sqrt(F) / np.tile(s, CTX) * u[:, None]
    words, scales = pack_weight(np.ascontiguousarray(w_l.T), "e4m3")
    b_l = bf(np.random.standard_normal(H) * 0.3 * u)
    W_bil = bf(np.random.standard_normal((NOUT, H, H)) * 0.2 / np.sqrt(H) / u[None, :, None])
    return {"x_l": x_l, "W_l_words": words, "W_l_scales": scales, "b_l": b_l, "W_bil": W_bil}


def reference(x_l, W_l_words, W_l_scales, b_l, W_bil):
    xq = mxq(f64(x_l), 2, "e4m3")
    hl = np.maximum(context_linear(xq, unpack_weight(W_l_words, W_l_scales, "e4m3"), (shift_down, shift_up)) + f64(b_l), 0.0)
    wb = f64(W_bil).transpose(1, 0, 2).reshape(H, NOUT * H)
    t = mxq(hl, 2, "e4m3") @ mxq(wb, 0, "e4m3")
    return t.reshape(B, N, NOUT, H)

@@ -1,0 +1,238 @@
+from contextlib import ExitStack
+
+import concourse.mybir as mybir
+from concourse.masks import make_identity
+
+F32 = mybir.dt.float32
+BF16 = mybir.dt.bfloat16
+I32 = mybir.dt.int32
+U32 = mybir.dt.uint32
+U8 = mybir.dt.uint8
+FP8X4 = mybir.dt.float8_e4m3fn_x4
+RELU = mybir.ActivationFunctionType.Relu
+
+P = 128
+PACK = 4
+BANK = 512
+
+SEQUENCES = 8
+POSITIONS = 512
+FEATURES = 512
+HIDDEN = 512
+MAPS = 2
+TAPS = 3
+TOKENS = SEQUENCES * POSITIONS
+BLOCKS = TOKENS // P
+SEGMENTS_PER_SEQUENCE = POSITIONS // BLOCKS
+SLOTS = BLOCKS + 2
+WINDOW = BANK // P
+WINDOWS = BLOCKS // WINDOW
+H_CHUNKS = HIDDEN // P
+X_WORDS = FEATURES // 2
+OUT_COLUMNS = MAPS * HIDDEN
+
+TAP_SLOT = (1, 0, 2)
+
+STEPS = WINDOWS * H_CHUNKS
+LAYER2_LAG = 6
+W_BIL_STEP = 2
+
+FLOPS = 2 * TOKENS * (TAPS * FEATURES * HIDDEN + HIDDEN * OUT_COLUMNS)
+
+
+def tile_bilinearpairedlayer_pa_t_kernel(tc, x_l, W_l_words, W_l_scales, b_l, W_bil, out):
+    nc = tc.nc
+    x_blocks = x_l.rearrange("b (s r) f -> (b s) r f", r=BLOCKS)
+    out_blocks = out.rearrange("b (s r) k g -> (b s) r (k g)", r=BLOCKS)
+
+    with ExitStack() as ctx:
+        ctx.enter_context(tc.manual_schedule())
+        keep = ctx.enter_context(tc.tile_pool(name="keep", bufs=1))
+        results = ctx.enter_context(tc.tile_pool(name="results", bufs=4))
+        psum_t = ctx.enter_context(tc.psum_pool(name="psum_t", bufs=2))
+        psum_1 = ctx.enter_context(tc.psum_pool(name="psum_1", bufs=2))
+        psum_2 = ctx.enter_context(tc.psum_pool(name="psum_2", bufs=4))
+
+        x_sb = keep.tile([P, BLOCKS, FEATURES], BF16)
+        x_last = keep.tile([P, FEATURES], BF16)
+        xq_words = keep.tile([P, SLOTS * P], U32, align_bytes=64)
+        xq_scales = keep.tile([P, SLOTS * P], U8, align_bytes=64)
+        w_words = keep.tile([P, TAPS, HIDDEN], U32, align_bytes=64)
+        w_scales = keep.tile([P, TAPS, HIDDEN], U8, align_bytes=64)
+        wb_raw = keep.tile([P, PACK, OUT_COLUMNS], BF16)
+        wb_grouped = keep.tile([P, OUT_COLUMNS, PACK], BF16, align_bytes=64)
+        wbq_words = keep.tile([P, OUT_COLUMNS], U32, align_bytes=64)
+        wbq_scales = keep.tile([P, OUT_COLUMNS], U8, align_bytes=64)
+        identity = keep.tile([P, P], F32)
+        to_next_segment = keep.tile([P, P], F32)
+        to_previous_segment = keep.tile([P, P], F32)
+        bias_rows = keep.tile([P, P], BF16)
+        bias_rows_f32 = keep.tile([P, P], F32)
+        bias = keep.tile([P, H_CHUNKS], F32)
+        x_grouped_ends = keep.tile([P, 2, P, PACK], BF16, align_bytes=64)
+        x_grouped = keep.tile([P, 2, WINDOW, P, PACK], BF16, align_bytes=64)
+        h_planes = keep.tile([P, 2, H_CHUNKS, BANK], BF16)
+        h_grouped = keep.tile([P, 2, BANK, PACK], BF16, align_bytes=64)
+        hq_words = keep.tile([P, 2, BANK], U32, align_bytes=64)
+        hq_scales = keep.tile([P, 2, BANK], U8, align_bytes=64)
+
+        nc.vector.memset(w_scales[:].bitcast(I32), 0)
+        nc.vector.memset(bias_rows[:], 0.0)
+        nc.vector.memset(to_next_segment[:], 0.0)
+        nc.vector.memset(to_previous_segment[:], 0.0)
+        make_identity(nc, identity[:])
+        by_sequence = "p (b s) -> p b s"
+        nc.vector.tensor_copy(
+            out=to_next_segment[:].rearrange(by_sequence, s=SEGMENTS_PER_SEQUENCE)[:, :, 1:],
+            in_=identity[:].rearrange(by_sequence, s=SEGMENTS_PER_SEQUENCE)[:, :, : SEGMENTS_PER_SEQUENCE - 1],
+        )
+        nc.vector.tensor_copy(
+            out=to_previous_segment[:].rearrange(by_sequence, s=SEGMENTS_PER_SEQUENCE)[:, :, : SEGMENTS_PER_SEQUENCE - 1],
+            in_=identity[:].rearrange(by_sequence, s=SEGMENTS_PER_SEQUENCE)[:, :, 1:],
+        )
+
+        def load_x_window(window):
+            blocks = slice(window * WINDOW, (window + 1) * WINDOW)
+            nc.sync.dma_start(out=x_sb[:, blocks, :], in_=x_blocks[:, blocks, :])
+
+        nc.sync.dma_start(out=x_last[:], in_=x_blocks[:, BLOCKS - 1, :])
+        load_x_window(0)
+        nc.sync.dma_start(out=bias_rows[0:H_CHUNKS, :], in_=b_l.rearrange("(t p) -> t p", p=P))
+        for quadrant in range(4):
+            nc.sync.dma_start(
+                out=w_scales[32 * quadrant : 32 * quadrant + 4, :, :].bitcast(I32),
+                in_=W_l_scales[:, 4 * quadrant : 4 * quadrant + 4, :].rearrange("g r n -> r g n").bitcast(I32),
+            )
+        load_x_window(1)
+        nc.sync.dma_start(
+            out=w_words[:].bitcast(I32),
+            in_=W_l_words.rearrange("g p n t -> p g (n t)").bitcast(I32),
+        )
+        load_x_window(2)
+        for k in range(MAPS):
+            nc.sync.dma_start(
+                out=wb_raw[:, :, k * HIDDEN : (k + 1) * HIDDEN],
+                in_=W_bil[k].rearrange("(t p) g -> p t g", p=P),
+            )
+        for window in range(3, WINDOWS):
+            load_x_window(window)
+
+        def transpose_block(bank_part, block_words, permutation):
+            for u in range(2):
+                nc.tensor.transpose(out=bank_part[:, u, :], in_=block_words[:, u:X_WORDS:2], identity=permutation)
+
+        def copy_pair_of_blocks(copy, grouped_pair, bank):
+            copy(out=grouped_pair.bitcast(F32), in_=bank[:].rearrange("p b u w -> p b w u"))
+
+        def quantise_x(first_slot, grouped):
+            width = grouped.shape[1] // PACK
+            columns = slice(first_slot * P, first_slot * P + width)
+            nc.vector.quantize_mx(out=xq_words[:, columns].bitcast(FP8X4), scales=xq_scales[:, columns], in_=grouped)
+
+        def transpose_window(window):
+            for half, copy in enumerate((nc.scalar.copy, nc.vector.tensor_copy)):
+                bank = psum_t.tile([P, 2, 2, P], F32, name="bank", tag="transposed")
+                for b in range(2):
+                    block = window * WINDOW + 2 * half + b
+                    transpose_block(bank[:, b], x_sb[:, block, :].bitcast(F32), identity[:])
+                copy_pair_of_blocks(copy, x_grouped[:, window % 2, 2 * half : 2 * half + 2], bank)
+
+        def quantise_window(window):
+            quantise_x(window * WINDOW + 1, x_grouped[:, window % 2].rearrange("p b w t -> p (b w t)"))
+
+        def layer1_group(window, chunk):
+            units = slice(chunk * P, (chunk + 1) * P)
+            group = psum_1.tile([P, BANK], F32, name="group")
+            for g in range(TAPS):
+                first = (window * WINDOW + TAP_SLOT[g]) * P
+                nc.tensor.matmul_mx(
+                    out=group[:],
+                    lhsT=w_words[:, g, units].bitcast(FP8X4),
+                    lhsT_scale=w_scales[:, g, units],
+                    rhs=xq_words[:, first : first + BANK].bitcast(FP8X4),
+                    rhs_scale=xq_scales[:, first : first + BANK],
+                    start=(g == 0),
+                    stop=(g == TAPS - 1),
+                )
+            nc.scalar.activation(
+                out=h_planes[:, window % 2, chunk, :], in_=group[:], func=RELU, bias=bias[:, chunk : chunk + 1], scale=1.0
+            )
+
+        def regroup(grouped, planes):
+            nc.vector.tensor_copy(
+                out=grouped.rearrange("p (c i) t -> p c t i", i=4), in_=planes.rearrange("p t (c i) -> p c t i", i=4)
+            )
+
+        def quantise_hidden(window):
+            nc.vector.quantize_mx(
+                out=hq_words[:, window % 2, :].bitcast(FP8X4),
+                scales=hq_scales[:, window % 2, :],
+                in_=h_grouped[:, window % 2].rearrange("p w t -> p (w t)"),
+            )
+
+        def layer2_block(block):
+            window, place = divmod(block, WINDOW)
+            tokens = slice(place * P, (place + 1) * P)
+            result = results.tile([P, OUT_COLUMNS], F32, name="result")
+            for k, copy in enumerate((nc.scalar.copy, nc.vector.tensor_copy)):
+                columns = slice(k * HIDDEN, (k + 1) * HIDDEN)
+                product = psum_2.tile([P, BANK], F32, name="product")
+                nc.tensor.matmul_mx(
+                    out=product[:],
+                    lhsT=hq_words[:, window % 2, tokens].bitcast(FP8X4),
+                    lhsT_scale=hq_scales[:, window % 2, tokens],
+                    rhs=wbq_words[:, columns].bitcast(FP8X4),
+                    rhs_scale=wbq_scales[:, columns],
+                    start=True,
+                    stop=True,
+                )
+                copy(out=result[:, columns], in_=product[:])
+            nc.sync.dma_start(out=out_blocks[:, block, :], in_=result[:])
+
+        def quantise_w_bil():
+            for k in range(MAPS):
+                columns = slice(k * HIDDEN, (k + 1) * HIDDEN)
+                regroup(wb_grouped[:, columns, :], wb_raw[:, :, columns])
+            for k in range(MAPS):
+                columns = slice(k * HIDDEN, (k + 1) * HIDDEN)
+                nc.vector.quantize_mx(
+                    out=wbq_words[:, columns].bitcast(FP8X4),
+                    scales=wbq_scales[:, columns],
+                    in_=wb_grouped[:, columns, :].rearrange("p n t -> p (n t)"),
+                )
+
+        ends = psum_t.tile([P, 2, 2, P], F32, name="ends", tag="transposed")
+        transpose_block(ends[:, 0], x_last[:].bitcast(F32), to_next_segment[:])
+        transpose_block(ends[:, 1], x_sb[:, 0, :].bitcast(F32), to_previous_segment[:])
+        copy_pair_of_blocks(nc.vector.tensor_copy, x_grouped_ends[:], ends)
+        transpose_window(0)
+        quantise_x(0, x_grouped_ends[:, 0].rearrange("p w t -> p (w t)"))
+        quantise_x(SLOTS - 1, x_grouped_ends[:, 1].rearrange("p w t -> p (w t)"))
+
+        nc.vector.tensor_copy(out=bias_rows_f32[:], in_=bias_rows[:])
+        bias_columns = psum_t.tile([P, P], F32, name="bias_columns", tag="transposed")
+        nc.tensor.transpose(out=bias_columns[:], in_=bias_rows_f32[:], identity=identity[:])
+        nc.vector.tensor_copy(out=bias[:], in_=bias_columns[:, 0:H_CHUNKS])
+
+        transpose_window(1)
+        quantise_window(0)
+        quantise_window(1)
+
+        for step in range(STEPS + LAYER2_LAG):
+            window, quarter = divmod(step, H_CHUNKS)
+            finished = window - 1
+            ahead = window + 2
+            if quarter == 0 and 0 <= finished < WINDOWS:
+                regroup(h_grouped[:, finished % 2], h_planes[:, finished % 2])
+            if quarter == 1 and 0 <= finished < WINDOWS:
+                quantise_hidden(finished)
+            if quarter == 1 and ahead < WINDOWS:
+                transpose_window(ahead)
+            if step == W_BIL_STEP:
+                quantise_w_bil()
+            if quarter == 3 and ahead < WINDOWS:
+                quantise_window(ahead)
+            if step < STEPS:
+                layer1_group(window, quarter)
+            if step >= LAYER2_LAG:
+                layer2_block(step - LAYER2_LAG)

@@ -46,7 +46,6 @@ def tile_bilinearpairedlayer_pa_t_kernel(tc, x_l, W_l_words, W_l_scales, b_l, W_
     out_blocks = out.rearrange("b (s r) k g -> (b s) r (k g)", r=BLOCKS)
 
     with ExitStack() as ctx:
-        ctx.enter_context(tc.manual_schedule())
         keep = ctx.enter_context(tc.tile_pool(name="keep", bufs=1))
         results = ctx.enter_context(tc.tile_pool(name="results", bufs=4))
         psum_t = ctx.enter_context(tc.psum_pool(name="psum_t", bufs=2))

@@ -25,7 +25,9 @@ TOKENS = SEQUENCES * POSITIONS
 BLOCKS = TOKENS // P
 SEGMENTS_PER_SEQUENCE = POSITIONS // BLOCKS
 SLOTS = BLOCKS + 2
-WINDOW = BANK // P
+PAIRS = SLOTS // 2
+WINDOW = 2
+WINDOW_TOKENS = WINDOW * P
 WINDOWS = BLOCKS // WINDOW
 H_CHUNKS = HIDDEN // P
 X_WORDS = FEATURES // 2
@@ -33,9 +35,14 @@ OUT_COLUMNS = MAPS * HIDDEN
 
 TAP_SLOT = (1, 0, 2)
 
-STEPS = WINDOWS * H_CHUNKS
-LAYER2_LAG = 6
-W_BIL_STEP = 2
+STEPS = 2 * WINDOWS
+LAYER2_LAG = 4
+FIRST_LAYER2_STEP = 5
+W_BIL_STEP = 1
+TRANSPOSE_EVERY = 4
+
+X_RING = 4
+HQ_RING = 4
 
 FLOPS = 2 * TOKENS * (TAPS * FEATURES * HIDDEN + HIDDEN * OUT_COLUMNS)
 
@@ -46,6 +53,7 @@ def tile_bilinearpairedlayer_pa_t_kernel(tc, x_l, W_l_words, W_l_scales, b_l, W_
     out_blocks = out.rearrange("b (s r) k g -> (b s) r (k g)", r=BLOCKS)
 
     with ExitStack() as ctx:
+        ctx.enter_context(tc.manual_schedule())
         keep = ctx.enter_context(tc.tile_pool(name="keep", bufs=1))
         results = ctx.enter_context(tc.tile_pool(name="results", bufs=4))
         psum_t = ctx.enter_context(tc.psum_pool(name="psum_t", bufs=2))
@@ -53,7 +61,6 @@ def tile_bilinearpairedlayer_pa_t_kernel(tc, x_l, W_l_words, W_l_scales, b_l, W_
         psum_2 = ctx.enter_context(tc.psum_pool(name="psum_2", bufs=4))
 
         x_sb = keep.tile([P, BLOCKS, FEATURES], BF16)
-        x_last = keep.tile([P, FEATURES], BF16)
         xq_words = keep.tile([P, SLOTS * P], U32, align_bytes=64)
         xq_scales = keep.tile([P, SLOTS * P], U8, align_bytes=64)
         w_words = keep.tile([P, TAPS, HIDDEN], U32, align_bytes=64)
@@ -68,12 +75,12 @@ def tile_bilinearpairedlayer_pa_t_kernel(tc, x_l, W_l_words, W_l_scales, b_l, W_
         bias_rows = keep.tile([P, P], BF16)
         bias_rows_f32 = keep.tile([P, P], F32)
         bias = keep.tile([P, H_CHUNKS], F32)
-        x_grouped_ends = keep.tile([P, 2, P, PACK], BF16, align_bytes=64)
-        x_grouped = keep.tile([P, 2, WINDOW, P, PACK], BF16, align_bytes=64)
-        h_planes = keep.tile([P, 2, H_CHUNKS, BANK], BF16)
-        h_grouped = keep.tile([P, 2, BANK, PACK], BF16, align_bytes=64)
-        hq_words = keep.tile([P, 2, BANK], U32, align_bytes=64)
-        hq_scales = keep.tile([P, 2, BANK], U8, align_bytes=64)
+        x_grouped = keep.tile([P, X_RING, 2, P, PACK], BF16, align_bytes=64)
+        h_planes = keep.tile([P, 2, H_CHUNKS, WINDOW_TOKENS], BF16)
+        h_grouped = keep.tile([P, 2, WINDOW_TOKENS, PACK], BF16, align_bytes=64)
+        hq_words = keep.tile([P, HQ_RING, WINDOW_TOKENS], U32, align_bytes=64)
+        hq_scales = keep.tile([P, HQ_RING, WINDOW_TOKENS], U8, align_bytes=64)
+        x_words = x_sb[:].bitcast(F32)
 
         nc.vector.memset(w_scales[:].bitcast(I32), 0)
         nc.vector.memset(bias_rows[:], 0.0)
@@ -90,72 +97,88 @@ def tile_bilinearpairedlayer_pa_t_kernel(tc, x_l, W_l_words, W_l_scales, b_l, W_
             in_=identity[:].rearrange(by_sequence, s=SEGMENTS_PER_SEQUENCE)[:, :, 1:],
         )
 
-        def load_x_window(window):
-            blocks = slice(window * WINDOW, (window + 1) * WINDOW)
+        def load_blocks(blocks):
             nc.sync.dma_start(out=x_sb[:, blocks, :], in_=x_blocks[:, blocks, :])
 
-        nc.sync.dma_start(out=x_last[:], in_=x_blocks[:, BLOCKS - 1, :])
-        load_x_window(0)
+        def load_pair(pair):
+            load_blocks(slice(2 * pair - 1, 2 * pair + 1))
+
+        def load_weight_half(half):
+            units = slice(half * HIDDEN // 2, (half + 1) * HIDDEN // 2)
+            nc.sync.dma_start(
+                out=w_words[:, :, units].bitcast(I32),
+                in_=W_l_words.rearrange("g p n t -> p g (n t)").bitcast(I32)[:, :, units],
+            )
+
+        load_blocks(slice(0, BLOCKS, BLOCKS - 1))
+        load_pair(1)
         nc.sync.dma_start(out=bias_rows[0:H_CHUNKS, :], in_=b_l.rearrange("(t p) -> t p", p=P))
         for quadrant in range(4):
             nc.sync.dma_start(
                 out=w_scales[32 * quadrant : 32 * quadrant + 4, :, :].bitcast(I32),
                 in_=W_l_scales[:, 4 * quadrant : 4 * quadrant + 4, :].rearrange("g r n -> r g n").bitcast(I32),
             )
-        load_x_window(1)
-        nc.sync.dma_start(
-            out=w_words[:].bitcast(I32),
-            in_=W_l_words.rearrange("g p n t -> p g (n t)").bitcast(I32),
-        )
-        load_x_window(2)
+        load_weight_half(0)
+        load_pair(2)
+        load_weight_half(1)
+        load_pair(3)
         for k in range(MAPS):
             nc.sync.dma_start(
                 out=wb_raw[:, :, k * HIDDEN : (k + 1) * HIDDEN],
                 in_=W_bil[k].rearrange("(t p) g -> p t g", p=P),
             )
-        for window in range(3, WINDOWS):
-            load_x_window(window)
+        for pair in range(4, PAIRS - 1):
+            load_pair(pair)
 
-        def transpose_block(bank_part, block_words, permutation):
-            for u in range(2):
-                nc.tensor.transpose(out=bank_part[:, u, :], in_=block_words[:, u:X_WORDS:2], identity=permutation)
+        def slot_source(slot):
+            if slot == 0:
+                return BLOCKS - 1, to_next_segment
+            if slot == SLOTS - 1:
+                return 0, to_previous_segment
+            return slot - 1, identity
 
-        def copy_pair_of_blocks(copy, grouped_pair, bank):
-            copy(out=grouped_pair.bitcast(F32), in_=bank[:].rearrange("p b u w -> p b w u"))
+        def transpose_pair(pair):
+            bank = psum_t.tile([P, 2, 2, P], F32, name="bank", tag="transposed")
+            for b in range(2):
+                block, permutation = slot_source(2 * pair + b)
+                for u in range(2):
+                    nc.tensor.transpose(out=bank[:, b, u, :], in_=x_words[:, block, u:X_WORDS:2], identity=permutation[:])
+            copy = nc.scalar.copy if pair % 2 else nc.vector.tensor_copy
+            copy(out=x_grouped[:, pair % X_RING].bitcast(F32), in_=bank[:].rearrange("p b u w -> p b w u"))
 
-        def quantise_x(first_slot, grouped):
-            width = grouped.shape[1] // PACK
-            columns = slice(first_slot * P, first_slot * P + width)
-            nc.vector.quantize_mx(out=xq_words[:, columns].bitcast(FP8X4), scales=xq_scales[:, columns], in_=grouped)
-
-        def transpose_window(window):
-            for half, copy in enumerate((nc.scalar.copy, nc.vector.tensor_copy)):
-                bank = psum_t.tile([P, 2, 2, P], F32, name="bank", tag="transposed")
-                for b in range(2):
-                    block = window * WINDOW + 2 * half + b
-                    transpose_block(bank[:, b], x_sb[:, block, :].bitcast(F32), identity[:])
-                copy_pair_of_blocks(copy, x_grouped[:, window % 2, 2 * half : 2 * half + 2], bank)
-
-        def quantise_window(window):
-            quantise_x(window * WINDOW + 1, x_grouped[:, window % 2].rearrange("p b w t -> p (b w t)"))
-
-        def layer1_group(window, chunk):
-            units = slice(chunk * P, (chunk + 1) * P)
-            group = psum_1.tile([P, BANK], F32, name="group")
-            for g in range(TAPS):
-                first = (window * WINDOW + TAP_SLOT[g]) * P
-                nc.tensor.matmul_mx(
-                    out=group[:],
-                    lhsT=w_words[:, g, units].bitcast(FP8X4),
-                    lhsT_scale=w_scales[:, g, units],
-                    rhs=xq_words[:, first : first + BANK].bitcast(FP8X4),
-                    rhs_scale=xq_scales[:, first : first + BANK],
-                    start=(g == 0),
-                    stop=(g == TAPS - 1),
-                )
-            nc.scalar.activation(
-                out=h_planes[:, window % 2, chunk, :], in_=group[:], func=RELU, bias=bias[:, chunk : chunk + 1], scale=1.0
+        def quantise_pair(pair):
+            columns = slice(2 * pair * P, (2 * pair + 2) * P)
+            nc.vector.quantize_mx(
+                out=xq_words[:, columns].bitcast(FP8X4),
+                scales=xq_scales[:, columns],
+                in_=x_grouped[:, pair % X_RING].rearrange("p b w t -> p (b w t)"),
             )
+
+        def layer1_bank(window, half):
+            groups = psum_1.tile([P, 2, WINDOW_TOKENS], F32, name="groups")
+            for i in range(2):
+                chunk = 2 * half + i
+                units = slice(chunk * P, (chunk + 1) * P)
+                for g in range(TAPS):
+                    first = (window * WINDOW + TAP_SLOT[g]) * P
+                    nc.tensor.matmul_mx(
+                        out=groups[:, i, :],
+                        lhsT=w_words[:, g, units].bitcast(FP8X4),
+                        lhsT_scale=w_scales[:, g, units],
+                        rhs=xq_words[:, first : first + WINDOW_TOKENS].bitcast(FP8X4),
+                        rhs_scale=xq_scales[:, first : first + WINDOW_TOKENS],
+                        start=(g == 0),
+                        stop=(g == TAPS - 1),
+                    )
+            for i in range(2):
+                chunk = 2 * half + i
+                nc.scalar.activation(
+                    out=h_planes[:, window % 2, chunk, :],
+                    in_=groups[:, i, :],
+                    func=RELU,
+                    bias=bias[:, chunk : chunk + 1],
+                    scale=1.0,
+                )
 
         def regroup(grouped, planes):
             nc.vector.tensor_copy(
@@ -164,29 +187,10 @@ def tile_bilinearpairedlayer_pa_t_kernel(tc, x_l, W_l_words, W_l_scales, b_l, W_
 
         def quantise_hidden(window):
             nc.vector.quantize_mx(
-                out=hq_words[:, window % 2, :].bitcast(FP8X4),
-                scales=hq_scales[:, window % 2, :],
+                out=hq_words[:, window % HQ_RING, :].bitcast(FP8X4),
+                scales=hq_scales[:, window % HQ_RING, :],
                 in_=h_grouped[:, window % 2].rearrange("p w t -> p (w t)"),
             )
-
-        def layer2_block(block):
-            window, place = divmod(block, WINDOW)
-            tokens = slice(place * P, (place + 1) * P)
-            result = results.tile([P, OUT_COLUMNS], F32, name="result")
-            for k, copy in enumerate((nc.scalar.copy, nc.vector.tensor_copy)):
-                columns = slice(k * HIDDEN, (k + 1) * HIDDEN)
-                product = psum_2.tile([P, BANK], F32, name="product")
-                nc.tensor.matmul_mx(
-                    out=product[:],
-                    lhsT=hq_words[:, window % 2, tokens].bitcast(FP8X4),
-                    lhsT_scale=hq_scales[:, window % 2, tokens],
-                    rhs=wbq_words[:, columns].bitcast(FP8X4),
-                    rhs_scale=wbq_scales[:, columns],
-                    start=True,
-                    stop=True,
-                )
-                copy(out=result[:, columns], in_=product[:])
-            nc.sync.dma_start(out=out_blocks[:, block, :], in_=result[:])
 
         def quantise_w_bil():
             for k in range(MAPS):
@@ -200,38 +204,52 @@ def tile_bilinearpairedlayer_pa_t_kernel(tc, x_l, W_l_words, W_l_scales, b_l, W_
                     in_=wb_grouped[:, columns, :].rearrange("p n t -> p (n t)"),
                 )
 
-        ends = psum_t.tile([P, 2, 2, P], F32, name="ends", tag="transposed")
-        transpose_block(ends[:, 0], x_last[:].bitcast(F32), to_next_segment[:])
-        transpose_block(ends[:, 1], x_sb[:, 0, :].bitcast(F32), to_previous_segment[:])
-        copy_pair_of_blocks(nc.vector.tensor_copy, x_grouped_ends[:], ends)
-        transpose_window(0)
-        quantise_x(0, x_grouped_ends[:, 0].rearrange("p w t -> p (w t)"))
-        quantise_x(SLOTS - 1, x_grouped_ends[:, 1].rearrange("p w t -> p (w t)"))
+        def layer2_block(block):
+            window, place = divmod(block, WINDOW)
+            tokens = slice(place * P, (place + 1) * P)
+            result = results.tile([P, OUT_COLUMNS], F32, name="result")
+            for k, copy in enumerate((nc.scalar.copy, nc.vector.tensor_copy)):
+                columns = slice(k * HIDDEN, (k + 1) * HIDDEN)
+                product = psum_2.tile([P, BANK], F32, name="product")
+                nc.tensor.matmul_mx(
+                    out=product[:],
+                    lhsT=hq_words[:, window % HQ_RING, tokens].bitcast(FP8X4),
+                    lhsT_scale=hq_scales[:, window % HQ_RING, tokens],
+                    rhs=wbq_words[:, columns].bitcast(FP8X4),
+                    rhs_scale=wbq_scales[:, columns],
+                    start=True,
+                    stop=True,
+                )
+                copy(out=result[:, columns], in_=product[:])
+            nc.sync.dma_start(out=out_blocks[:, block, :], in_=result[:])
 
         nc.vector.tensor_copy(out=bias_rows_f32[:], in_=bias_rows[:])
+        transpose_pair(0)
         bias_columns = psum_t.tile([P, P], F32, name="bias_columns", tag="transposed")
         nc.tensor.transpose(out=bias_columns[:], in_=bias_rows_f32[:], identity=identity[:])
         nc.vector.tensor_copy(out=bias[:], in_=bias_columns[:, 0:H_CHUNKS])
+        transpose_pair(1)
+        quantise_pair(0)
+        quantise_pair(1)
 
-        transpose_window(1)
-        quantise_window(0)
-        quantise_window(1)
-
+        next_block = 0
         for step in range(STEPS + LAYER2_LAG):
-            window, quarter = divmod(step, H_CHUNKS)
+            window, half = divmod(step, 2)
             finished = window - 1
-            ahead = window + 2
-            if quarter == 0 and 0 <= finished < WINDOWS:
+            if half == 0 and 0 <= finished < WINDOWS:
                 regroup(h_grouped[:, finished % 2], h_planes[:, finished % 2])
-            if quarter == 1 and 0 <= finished < WINDOWS:
+            if half == 1 and 0 <= finished < WINDOWS:
                 quantise_hidden(finished)
-            if quarter == 1 and ahead < WINDOWS:
-                transpose_window(ahead)
+            run = [pair for pair in (step // 2 + 2, step // 2 + 3) if step % TRANSPOSE_EVERY == 0 and pair < PAIRS]
+            for pair in run:
+                transpose_pair(pair)
             if step == W_BIL_STEP:
                 quantise_w_bil()
-            if quarter == 3 and ahead < WINDOWS:
-                quantise_window(ahead)
             if step < STEPS:
-                layer1_group(window, quarter)
-            if step >= LAYER2_LAG:
-                layer2_block(step - LAYER2_LAG)
+                layer1_bank(window, half)
+            for turn in range(2):
+                if step >= FIRST_LAYER2_STEP and next_block < BLOCKS and next_block + LAYER2_LAG <= step:
+                    layer2_block(next_block)
+                    next_block += 1
+            for pair in run:
+                quantise_pair(pair)

@@ -37,12 +37,9 @@ TAP_SLOT = (1, 0, 2)
 
 STEPS = 2 * WINDOWS
 LAYER2_LAG = 4
-FIRST_LAYER2_STEP = 5
-W_BIL_STEP = 1
 TRANSPOSE_EVERY = 4
-
-X_RING = 4
-HQ_RING = 4
+PAIRS_IN_A_RUN = 2
+W_BIL_STEP = 1
 
 FLOPS = 2 * TOKENS * (TAPS * FEATURES * HIDDEN + HIDDEN * OUT_COLUMNS)
 
@@ -75,11 +72,11 @@ def tile_bilinearpairedlayer_pa_t_kernel(tc, x_l, W_l_words, W_l_scales, b_l, W_
         bias_rows = keep.tile([P, P], BF16)
         bias_rows_f32 = keep.tile([P, P], F32)
         bias = keep.tile([P, H_CHUNKS], F32)
-        x_grouped = keep.tile([P, X_RING, 2, P, PACK], BF16, align_bytes=64)
+        x_grouped = keep.tile([P, 2, 2, P, PACK], BF16, align_bytes=64)
         h_planes = keep.tile([P, 2, H_CHUNKS, WINDOW_TOKENS], BF16)
         h_grouped = keep.tile([P, 2, WINDOW_TOKENS, PACK], BF16, align_bytes=64)
-        hq_words = keep.tile([P, HQ_RING, WINDOW_TOKENS], U32, align_bytes=64)
-        hq_scales = keep.tile([P, HQ_RING, WINDOW_TOKENS], U8, align_bytes=64)
+        hq_words = keep.tile([P, 2, WINDOW_TOKENS], U32, align_bytes=64)
+        hq_scales = keep.tile([P, 2, WINDOW_TOKENS], U8, align_bytes=64)
         x_words = x_sb[:].bitcast(F32)
 
         nc.vector.memset(w_scales[:].bitcast(I32), 0)
@@ -144,14 +141,14 @@ def tile_bilinearpairedlayer_pa_t_kernel(tc, x_l, W_l_words, W_l_scales, b_l, W_
                 for u in range(2):
                     nc.tensor.transpose(out=bank[:, b, u, :], in_=x_words[:, block, u:X_WORDS:2], identity=permutation[:])
             copy = nc.scalar.copy if pair % 2 else nc.vector.tensor_copy
-            copy(out=x_grouped[:, pair % X_RING].bitcast(F32), in_=bank[:].rearrange("p b u w -> p b w u"))
+            copy(out=x_grouped[:, pair % 2].bitcast(F32), in_=bank[:].rearrange("p b u w -> p b w u"))
 
         def quantise_pair(pair):
             columns = slice(2 * pair * P, (2 * pair + 2) * P)
             nc.vector.quantize_mx(
                 out=xq_words[:, columns].bitcast(FP8X4),
                 scales=xq_scales[:, columns],
-                in_=x_grouped[:, pair % X_RING].rearrange("p b w t -> p (b w t)"),
+                in_=x_grouped[:, pair % 2].rearrange("p b w t -> p (b w t)"),
             )
 
         def layer1_bank(window, half):
@@ -187,8 +184,8 @@ def tile_bilinearpairedlayer_pa_t_kernel(tc, x_l, W_l_words, W_l_scales, b_l, W_
 
         def quantise_hidden(window):
             nc.vector.quantize_mx(
-                out=hq_words[:, window % HQ_RING, :].bitcast(FP8X4),
-                scales=hq_scales[:, window % HQ_RING, :],
+                out=hq_words[:, window % 2, :].bitcast(FP8X4),
+                scales=hq_scales[:, window % 2, :],
                 in_=h_grouped[:, window % 2].rearrange("p w t -> p (w t)"),
             )
 
@@ -213,8 +210,8 @@ def tile_bilinearpairedlayer_pa_t_kernel(tc, x_l, W_l_words, W_l_scales, b_l, W_
                 product = psum_2.tile([P, BANK], F32, name="product")
                 nc.tensor.matmul_mx(
                     out=product[:],
-                    lhsT=hq_words[:, window % HQ_RING, tokens].bitcast(FP8X4),
-                    lhsT_scale=hq_scales[:, window % HQ_RING, tokens],
+                    lhsT=hq_words[:, window % 2, tokens].bitcast(FP8X4),
+                    lhsT_scale=hq_scales[:, window % 2, tokens],
                     rhs=wbq_words[:, columns].bitcast(FP8X4),
                     rhs_scale=wbq_scales[:, columns],
                     start=True,
@@ -232,7 +229,6 @@ def tile_bilinearpairedlayer_pa_t_kernel(tc, x_l, W_l_words, W_l_scales, b_l, W_
         quantise_pair(0)
         quantise_pair(1)
 
-        next_block = 0
         for step in range(STEPS + LAYER2_LAG):
             window, half = divmod(step, 2)
             finished = window - 1
@@ -240,16 +236,16 @@ def tile_bilinearpairedlayer_pa_t_kernel(tc, x_l, W_l_words, W_l_scales, b_l, W_
                 regroup(h_grouped[:, finished % 2], h_planes[:, finished % 2])
             if half == 1 and 0 <= finished < WINDOWS:
                 quantise_hidden(finished)
-            run = [pair for pair in (step // 2 + 2, step // 2 + 3) if step % TRANSPOSE_EVERY == 0 and pair < PAIRS]
+            run = ()
+            if step % TRANSPOSE_EVERY == 0:
+                run = range(window + 2, min(window + 2 + PAIRS_IN_A_RUN, PAIRS))
             for pair in run:
                 transpose_pair(pair)
             if step == W_BIL_STEP:
                 quantise_w_bil()
             if step < STEPS:
                 layer1_bank(window, half)
-            for turn in range(2):
-                if step >= FIRST_LAYER2_STEP and next_block < BLOCKS and next_block + LAYER2_LAG <= step:
-                    layer2_block(next_block)
-                    next_block += 1
+            if step >= LAYER2_LAG:
+                layer2_block(step - LAYER2_LAG)
             for pair in run:
                 quantise_pair(pair)

from contextlib import ExitStack

import concourse.mybir as mybir
from concourse.masks import make_identity

F32 = mybir.dt.float32
BF16 = mybir.dt.bfloat16
I32 = mybir.dt.int32
U32 = mybir.dt.uint32
U8 = mybir.dt.uint8
FP8X4 = mybir.dt.float8_e4m3fn_x4
RELU = mybir.ActivationFunctionType.Relu

P = 128
PACK = 4
BANK = 512

SEQUENCES = 8
POSITIONS = 512
FEATURES = 512
HIDDEN = 512
MAPS = 2
TAPS = 3
TOKENS = SEQUENCES * POSITIONS
BLOCKS = TOKENS // P
SEGMENTS_PER_SEQUENCE = POSITIONS // BLOCKS
SLOTS = BLOCKS + 2
PAIRS = SLOTS // 2
WINDOW = 2
WINDOW_TOKENS = WINDOW * P
WINDOWS = BLOCKS // WINDOW
H_CHUNKS = HIDDEN // P
X_WORDS = FEATURES // 2
OUT_COLUMNS = MAPS * HIDDEN

TAP_SLOT = (1, 0, 2)

STEPS = 2 * WINDOWS
LAYER2_LAG = 4
TRANSPOSE_EVERY = 4
PAIRS_IN_A_RUN = 2
W_BIL_STEP = 1

FLOPS = 2 * TOKENS * (TAPS * FEATURES * HIDDEN + HIDDEN * OUT_COLUMNS)


def tile_bilinearpairedlayer_pa_t_kernel(tc, x_l, W_l_words, W_l_scales, b_l, W_bil, out):
    nc = tc.nc
    x_blocks = x_l.rearrange("b (s r) f -> (b s) r f", r=BLOCKS)
    out_blocks = out.rearrange("b (s r) k g -> (b s) r (k g)", r=BLOCKS)

    with ExitStack() as ctx:
        ctx.enter_context(tc.manual_schedule())
        keep = ctx.enter_context(tc.tile_pool(name="keep", bufs=1))
        results = ctx.enter_context(tc.tile_pool(name="results", bufs=4))
        psum_t = ctx.enter_context(tc.psum_pool(name="psum_t", bufs=2))
        psum_1 = ctx.enter_context(tc.psum_pool(name="psum_1", bufs=2))
        psum_2 = ctx.enter_context(tc.psum_pool(name="psum_2", bufs=4))

        x_sb = keep.tile([P, BLOCKS, FEATURES], BF16)
        xq_words = keep.tile([P, SLOTS * P], U32, align_bytes=64)
        xq_scales = keep.tile([P, SLOTS * P], U8, align_bytes=64)
        w_words = keep.tile([P, TAPS, HIDDEN], U32, align_bytes=64)
        w_scales = keep.tile([P, TAPS, HIDDEN], U8, align_bytes=64)
        wb_raw = keep.tile([P, PACK, OUT_COLUMNS], BF16)
        wb_grouped = keep.tile([P, OUT_COLUMNS, PACK], BF16, align_bytes=64)
        wbq_words = keep.tile([P, OUT_COLUMNS], U32, align_bytes=64)
        wbq_scales = keep.tile([P, OUT_COLUMNS], U8, align_bytes=64)
        identity = keep.tile([P, P], F32)
        to_next_segment = keep.tile([P, P], F32)
        to_previous_segment = keep.tile([P, P], F32)
        bias_rows = keep.tile([P, P], BF16)
        bias_rows_f32 = keep.tile([P, P], F32)
        bias = keep.tile([P, H_CHUNKS], F32)
        x_grouped = keep.tile([P, 2, 2, P, PACK], BF16, align_bytes=64)
        h_planes = keep.tile([P, 2, H_CHUNKS, WINDOW_TOKENS], BF16)
        h_grouped = keep.tile([P, 2, WINDOW_TOKENS, PACK], BF16, align_bytes=64)
        hq_words = keep.tile([P, 2, WINDOW_TOKENS], U32, align_bytes=64)
        hq_scales = keep.tile([P, 2, WINDOW_TOKENS], U8, align_bytes=64)
        x_words = x_sb[:].bitcast(F32)

        nc.vector.memset(w_scales[:].bitcast(I32), 0)
        nc.vector.memset(bias_rows[:], 0.0)
        nc.vector.memset(to_next_segment[:], 0.0)
        nc.vector.memset(to_previous_segment[:], 0.0)
        make_identity(nc, identity[:])
        by_sequence = "p (b s) -> p b s"
        nc.vector.tensor_copy(
            out=to_next_segment[:].rearrange(by_sequence, s=SEGMENTS_PER_SEQUENCE)[:, :, 1:],
            in_=identity[:].rearrange(by_sequence, s=SEGMENTS_PER_SEQUENCE)[:, :, : SEGMENTS_PER_SEQUENCE - 1],
        )
        nc.vector.tensor_copy(
            out=to_previous_segment[:].rearrange(by_sequence, s=SEGMENTS_PER_SEQUENCE)[:, :, : SEGMENTS_PER_SEQUENCE - 1],
            in_=identity[:].rearrange(by_sequence, s=SEGMENTS_PER_SEQUENCE)[:, :, 1:],
        )

        def load_blocks(blocks):
            nc.sync.dma_start(out=x_sb[:, blocks, :], in_=x_blocks[:, blocks, :])

        def load_pair(pair):
            load_blocks(slice(2 * pair - 1, 2 * pair + 1))

        def load_weight_half(half):
            units = slice(half * HIDDEN // 2, (half + 1) * HIDDEN // 2)
            nc.sync.dma_start(
                out=w_words[:, :, units].bitcast(I32),
                in_=W_l_words.rearrange("g p n t -> p g (n t)").bitcast(I32)[:, :, units],
            )

        load_blocks(slice(0, BLOCKS, BLOCKS - 1))
        load_pair(1)
        nc.sync.dma_start(out=bias_rows[0:H_CHUNKS, :], in_=b_l.rearrange("(t p) -> t p", p=P))
        for quadrant in range(4):
            nc.sync.dma_start(
                out=w_scales[32 * quadrant : 32 * quadrant + 4, :, :].bitcast(I32),
                in_=W_l_scales[:, 4 * quadrant : 4 * quadrant + 4, :].rearrange("g r n -> r g n").bitcast(I32),
            )
        load_weight_half(0)
        load_pair(2)
        load_weight_half(1)
        load_pair(3)
        for k in range(MAPS):
            nc.sync.dma_start(
                out=wb_raw[:, :, k * HIDDEN : (k + 1) * HIDDEN],
                in_=W_bil[k].rearrange("(t p) g -> p t g", p=P),
            )
        for pair in range(4, PAIRS - 1):
            load_pair(pair)

        def slot_source(slot):
            if slot == 0:
                return BLOCKS - 1, to_next_segment
            if slot == SLOTS - 1:
                return 0, to_previous_segment
            return slot - 1, identity

        def transpose_pair(pair):
            bank = psum_t.tile([P, 2, 2, P], F32, name="bank", tag="transposed")
            for b in range(2):
                block, permutation = slot_source(2 * pair + b)
                for u in range(2):
                    nc.tensor.transpose(out=bank[:, b, u, :], in_=x_words[:, block, u:X_WORDS:2], identity=permutation[:])
            copy = nc.scalar.copy if pair % 2 else nc.vector.tensor_copy
            copy(out=x_grouped[:, pair % 2].bitcast(F32), in_=bank[:].rearrange("p b u w -> p b w u"))

        def quantise_pair(pair):
            columns = slice(2 * pair * P, (2 * pair + 2) * P)
            nc.vector.quantize_mx(
                out=xq_words[:, columns].bitcast(FP8X4),
                scales=xq_scales[:, columns],
                in_=x_grouped[:, pair % 2].rearrange("p b w t -> p (b w t)"),
            )

        def layer1_bank(window, half):
            groups = psum_1.tile([P, 2, WINDOW_TOKENS], F32, name="groups")
            for i in range(2):
                chunk = 2 * half + i
                units = slice(chunk * P, (chunk + 1) * P)
                for g in range(TAPS):
                    first = (window * WINDOW + TAP_SLOT[g]) * P
                    nc.tensor.matmul_mx(
                        out=groups[:, i, :],
                        lhsT=w_words[:, g, units].bitcast(FP8X4),
                        lhsT_scale=w_scales[:, g, units],
                        rhs=xq_words[:, first : first + WINDOW_TOKENS].bitcast(FP8X4),
                        rhs_scale=xq_scales[:, first : first + WINDOW_TOKENS],
                        start=(g == 0),
                        stop=(g == TAPS - 1),
                    )
            for i in range(2):
                chunk = 2 * half + i
                nc.scalar.activation(
                    out=h_planes[:, window % 2, chunk, :],
                    in_=groups[:, i, :],
                    func=RELU,
                    bias=bias[:, chunk : chunk + 1],
                    scale=1.0,
                )

        def regroup(grouped, planes):
            nc.vector.tensor_copy(
                out=grouped.rearrange("p (c i) t -> p c t i", i=4), in_=planes.rearrange("p t (c i) -> p c t i", i=4)
            )

        def quantise_hidden(window):
            nc.vector.quantize_mx(
                out=hq_words[:, window % 2, :].bitcast(FP8X4),
                scales=hq_scales[:, window % 2, :],
                in_=h_grouped[:, window % 2].rearrange("p w t -> p (w t)"),
            )

        def quantise_w_bil():
            for k in range(MAPS):
                columns = slice(k * HIDDEN, (k + 1) * HIDDEN)
                regroup(wb_grouped[:, columns, :], wb_raw[:, :, columns])
            for k in range(MAPS):
                columns = slice(k * HIDDEN, (k + 1) * HIDDEN)
                nc.vector.quantize_mx(
                    out=wbq_words[:, columns].bitcast(FP8X4),
                    scales=wbq_scales[:, columns],
                    in_=wb_grouped[:, columns, :].rearrange("p n t -> p (n t)"),
                )

        def layer2_block(block):
            window, place = divmod(block, WINDOW)
            tokens = slice(place * P, (place + 1) * P)
            result = results.tile([P, OUT_COLUMNS], F32, name="result")
            for k, copy in enumerate((nc.scalar.copy, nc.vector.tensor_copy)):
                columns = slice(k * HIDDEN, (k + 1) * HIDDEN)
                product = psum_2.tile([P, BANK], F32, name="product")
                nc.tensor.matmul_mx(
                    out=product[:],
                    lhsT=hq_words[:, window % 2, tokens].bitcast(FP8X4),
                    lhsT_scale=hq_scales[:, window % 2, tokens],
                    rhs=wbq_words[:, columns].bitcast(FP8X4),
                    rhs_scale=wbq_scales[:, columns],
                    start=True,
                    stop=True,
                )
                copy(out=result[:, columns], in_=product[:])
            nc.sync.dma_start(out=out_blocks[:, block, :], in_=result[:])

        nc.vector.tensor_copy(out=bias_rows_f32[:], in_=bias_rows[:])
        transpose_pair(0)
        bias_columns = psum_t.tile([P, P], F32, name="bias_columns", tag="transposed")
        nc.tensor.transpose(out=bias_columns[:], in_=bias_rows_f32[:], identity=identity[:])
        nc.vector.tensor_copy(out=bias[:], in_=bias_columns[:, 0:H_CHUNKS])
        transpose_pair(1)
        quantise_pair(0)
        quantise_pair(1)

        for step in range(STEPS + LAYER2_LAG):
            window, half = divmod(step, 2)
            finished = window - 1
            if half == 0 and 0 <= finished < WINDOWS:
                regroup(h_grouped[:, finished % 2], h_planes[:, finished % 2])
            if half == 1 and 0 <= finished < WINDOWS:
                quantise_hidden(finished)
            run = ()
            if step % TRANSPOSE_EVERY == 0:
                run = range(window + 2, min(window + 2 + PAIRS_IN_A_RUN, PAIRS))
            for pair in run:
                transpose_pair(pair)
            if step == W_BIL_STEP:
                quantise_w_bil()
            if step < STEPS:
                layer1_bank(window, half)
            if step >= LAYER2_LAG:
                layer2_block(step - LAYER2_LAG)
            for pair in run:
                quantise_pair(pair)
